import numpy as np
import ml_dtypes


def mxq(x, axis, fmt="e4m3"):
    dtype, down = {"e4m3": (ml_dtypes.float8_e4m3fn, 7), "e5m2": (ml_dtypes.float8_e5m2, 14)}[fmt]
    v = np.moveaxis(np.asarray(x, np.float32).astype(ml_dtypes.bfloat16).astype(np.float64), axis, -1)
    blocks = v.reshape(v.shape[:-1] + (-1, 32))
    amax = np.abs(blocks).max(-1, keepdims=True)
    byte = np.maximum(np.where(amax > 0, np.frexp(amax)[1] - 1 + 127, 0) - down, 1)
    scale = np.exp2(byte - 127.0)
    codes = (blocks / scale).astype(np.float32).astype(dtype).astype(np.float64)
    return np.moveaxis((codes * scale).reshape(v.shape), -1, axis)


WIDE = False


def mx_kscale(k):
    if not WIDE:
        return np.ones(k)
    levels = np.array([10, -10, 5, -5, 0])
    if k % 512:
        return np.exp2(np.random.permutation(np.resize(levels, k // 32))).repeat(32)
    a = np.empty((k // 512, 16))
    for p in range(k // 512):
        a[p, :8] = np.random.permutation(np.resize(levels, 8))
        for g in range(8):
            far = levels[np.abs(levels - a[p, g]) >= 10]
            a[p, g + 8] = far[np.random.randint(len(far))]
    return np.exp2(a.ravel()).repeat(32)


BF16 = ml_dtypes.bfloat16


def bf(x):
    return np.asarray(x, np.float32).astype(BF16)


def f64(x):
    return np.asarray(x).astype(np.float64)


E2M1 = np.array([0.0, 0.5, 1.0, 1.5, 2.0, 3.0, 4.0, 6.0, -0.0, -0.5, -1.0, -1.5, -2.0, -3.0, -4.0, -6.0])


def pack_weight(w, fmt):
    k, n = w.shape
    w = f64(bf(w)).reshape(k // 32, 32, n)
    amax = np.abs(w).max(1)
    if fmt == "e4m3":
        byte = np.frexp(amax)[1] - 1 + 127 - 7
    else:
        mant, ex = np.frexp(amax / 6.0)
        byte = np.where(mant > 0.5, ex, ex - 1) + 127
    byte = np.clip(np.where(amax > 0, byte, 1), 1, 254)
    scaled = (w * np.exp2(127.0 - byte)[:, None, :]).reshape(k, n).astype(np.float32)
    by_word = np.ascontiguousarray(scaled.reshape(k // 512, 128, 4, n).transpose(0, 1, 3, 2))
    if fmt == "e4m3":
        words = by_word.astype(ml_dtypes.float8_e4m3fn).view(np.uint8)
    else:
        c = by_word.astype(ml_dtypes.float4_e2m1fn).view(np.uint8) & 0xF
        words = c[..., 0::2] | (c[..., 1::2] << 4)
    return np.ascontiguousarray(words), np.ascontiguousarray(byte.astype(np.uint8).reshape(k // 512, 16, n))


def unpack_weight(words, scales, fmt):
    g, p, n, _ = words.shape
    if fmt == "e4m3":
        vals = np.ascontiguousarray(words).view(ml_dtypes.float8_e4m3fn).astype(np.float64)
    else:
        nib = np.empty((g, p, n, 4), np.uint8)
        nib[..., 0::2] = words & 0xF
        nib[..., 1::2] = words >> 4
        vals = E2M1[nib]
    vals = vals * np.repeat(np.exp2(scales.astype(np.float64) - 127.0), 8, axis=1)[..., None]
    return vals.transpose(0, 1, 3, 2).reshape(g * 512, n)
def pack4(w):
    words, scales = pack_weight(w, "e2m1")
    return words.reshape(words.shape[0], 128, -1), scales


def unpack4(words, scales):
    return unpack_weight(words.reshape(words.shape[0], 128, -1, 2), scales, "e2m1")


B, S, H, HD, LAT = 2, 2048, 4, 128, 512
HID = H * HD
ROT = HD // 2
HALF = ROT // 2
BASE = 10000.0


def make_rotary():
    inv_freq = 1.0 / BASE ** (np.arange(0, ROT, 2) / ROT)
    ang = np.arange(S)[:, None] * inv_freq[None, :]
    return np.concatenate([np.sin(ang), np.cos(ang)], axis=-1)[None, None, :, :]


def apply_rope(x, emb):
    x1, x2 = x[..., :HALF], x[..., HALF:]
    sin = emb[..., :HALF].transpose(0, 2, 1, 3)
    cos = emb[..., HALF:].transpose(0, 2, 1, 3)
    return np.concatenate([x1 * cos - x2 * sin, x1 * sin + x2 * cos], axis=-1)


def draw0():
    s, t = mx_kscale(HID), mx_kscale(LAT)
    hidden_states = bf(np.random.standard_normal((B, S, HID)) * s)
    rotary_emb = bf(make_rotary())
    W_kv_d_words, W_kv_d_scales = pack4(np.random.standard_normal((HID, LAT)) / np.sqrt(HID) / s[:, None] * t)
    W_k_u_words, W_k_u_scales = pack4(np.random.standard_normal((LAT, H * ROT)) / np.sqrt(LAT) / t[:, None])
    W_v_u_words, W_v_u_scales = pack4(np.random.standard_normal((LAT, H * HD)) / np.sqrt(LAT) / t[:, None])
    W_rope_k_words, W_rope_k_scales = pack4(np.random.standard_normal((HID, H * ROT)) / np.sqrt(HID) / s[:, None])
    return {"hidden_states": hidden_states,
            "rotary_emb": rotary_emb,
            "W_kv_d_words": W_kv_d_words,
            "W_kv_d_scales": W_kv_d_scales,
            "W_k_u_words": W_k_u_words,
            "W_k_u_scales": W_k_u_scales,
            "W_v_u_words": W_v_u_words,
            "W_v_u_scales": W_v_u_scales,
            "W_rope_k_words": W_rope_k_words,
            "W_rope_k_scales": W_rope_k_scales}


def core(hidden_states, rotary_emb, W_kv_d_words, W_kv_d_scales, W_k_u_words, W_k_u_scales, W_v_u_words, W_v_u_scales, W_rope_k_words, W_rope_k_scales):
    emb = f64(rotary_emb)
    xq = mxq(f64(hidden_states), 2, "e4m3")
    kv_d = xq @ unpack4(W_kv_d_words, W_kv_d_scales)
    kvq = mxq(kv_d, 2, "e4m3")
    k_c = (kvq @ unpack4(W_k_u_words, W_k_u_scales)).reshape(B, S, H, ROT)
    v = (kvq @ unpack4(W_v_u_words, W_v_u_scales)).reshape(B, S, H, HD)
    k_r = (xq @ unpack4(W_rope_k_words, W_rope_k_scales)).reshape(B, S, H, ROT)
    k_r = apply_rope(k_r, emb)
    k = np.concatenate([k_c, k_r], axis=-1)
    return k, v


def e4m3fn_bytes(y):
    return np.clip(np.asarray(y, np.float64), -448.0, 448.0).astype(np.float32).astype(ml_dtypes.float8_e4m3fn).view(np.uint8)


def e4m3fn_values(b):
    return np.asarray(b, np.uint8).view(ml_dtypes.float8_e4m3fn).astype(np.float64)


def setup_inputs():
    d = draw0()
    x0 = np.asarray(d['hidden_states']).astype(np.float64)
    s = (np.max(np.abs(x0), axis=(0, 1), keepdims=True) / 448.0).astype(np.float32)
    out = {}
    for k, v in d.items():
        if k == 'hidden_states':
            out['hidden_states_bytes'] = e4m3fn_bytes(x0 / s.astype(np.float64))
            out['hidden_states_scale'] = s
        else:
            out[k] = v
    return out


def reference(hidden_states_bytes, hidden_states_scale, rotary_emb, W_kv_d_words, W_kv_d_scales, W_k_u_words, W_k_u_scales, W_v_u_words, W_v_u_scales, W_rope_k_words, W_rope_k_scales):
    return core(e4m3fn_values(hidden_states_bytes) * hidden_states_scale.astype(np.float64), rotary_emb, W_kv_d_words, W_kv_d_scales, W_k_u_words, W_k_u_scales, W_v_u_words, W_v_u_scales, W_rope_k_words, W_rope_k_scales)

@@ -1,0 +1,267 @@
+from contextlib import ExitStack
+
+import concourse.mybir as mybir
+from concourse.masks import make_identity
+
+F32 = mybir.dt.float32
+BF16 = mybir.dt.bfloat16
+I32 = mybir.dt.int32
+U32 = mybir.dt.uint32
+U8 = mybir.dt.uint8
+FP8 = mybir.dt.float8_e4m3fn
+FP8X4 = mybir.dt.float8_e4m3fn_x4
+FP4X4 = mybir.dt.float4_e2m1fn_x4
+ADD = mybir.AluOpType.add
+SUB = mybir.AluOpType.subtract
+MULT = mybir.AluOpType.mult
+
+B, S, H, HD, HID, LAT = 2, 2048, 4, 128, 512, 512
+ROT, HALF = 64, 32
+P = 128
+R = S // P
+FLOPS = 2 * B * S * HID * (LAT + H * ROT + H * HD + H * ROT)
+
+PAIR = 2
+NP = B * R // PAIR
+SCALAR_WIDENS = (1, 2, 3, 5, 7, 9, 11, 13)
+VECTOR_COPIES = {("kc", 15, 0), ("v", 14, 0), ("v", 15, 0), ("k", 15, 0)}
+
+
+def tile_llamaattention_pb_t_w4_kernel(
+    tc, x_bytes, x_scale, emb, wkv_words, wkv_scales, wk_words, wk_scales,
+    wv_words, wv_scales, wr_words, wr_scales, k_out, v_out,
+):
+    nc = tc.nc
+    with ExitStack() as ctx:
+        keep = ctx.enter_context(tc.tile_pool(name="keep", bufs=1))
+        work = ctx.enter_context(tc.tile_pool(name="work", bufs=3))
+        psum = ctx.enter_context(tc.psum_pool(name="psum", bufs=1))
+        ctx.enter_context(tc.manual_schedule())
+
+        ident = keep.tile([P, P], F32)
+        make_identity(nc, ident[:])
+
+        planes = keep.tile([P, 1536], U8, align_bytes=64)
+        nc.vector.memset(planes[:].bitcast(I32), 0)
+        PL = {"kv": (0, 512), "v": (512, 1024), "k": (1024, 1280), "r": (1280, 1536)}
+
+        xb = [keep.tile([P, R, HID], U8, name="xb%d" % b) for b in range(B)]
+        x_view = [x_bytes[b].rearrange("(p r) k -> p r k", p=P) for b in range(B)]
+        xsc = keep.tile([P, 4], F32)
+        w_kv_raw = keep.tile([P, 1024], U8, align_bytes=64)
+        w_kv = keep.tile([P, 1024], U8, align_bytes=64)
+        s_kv = keep.tile([P, 512], U8, align_bytes=64)
+        w_v = keep.tile([P, 1024], U8, align_bytes=64)
+        w_k = keep.tile([P, 512], U8, align_bytes=64)
+        w_r = keep.tile([P, 512], U8, align_bytes=64)
+        embt = keep.tile([P, R, 2, HALF], BF16)
+
+        def load_x(b, r0, r1):
+            nc.sync.dma_start(out=xb[b][:, r0:r1, :], in_=x_view[b][:, r0:r1, :])
+
+        def load_words(tile, src):
+            nc.sync.dma_start(out=tile[:].bitcast(I32), in_=src[0].bitcast(I32))
+
+        def load_scales(which, src):
+            lo, hi = PL[which]
+            for q in range(4):
+                nc.sync.dma_start(
+                    out=planes[32 * q : 32 * q + 4, lo:hi].bitcast(I32),
+                    in_=src[0, 4 * q : 4 * q + 4, :].bitcast(I32),
+                )
+
+        load_x(0, 0, 2)
+        load_x(0, 2, 8)
+        nc.sync.dma_start(out=xsc[:], in_=x_scale.rearrange("a b (p t) -> p (a b t)", t=4))
+        load_words(w_kv_raw, wkv_words)
+        load_scales("kv", wkv_scales)
+        load_words(w_r, wr_words)
+        load_scales("r", wr_scales)
+        load_words(w_v, wv_words)
+        load_scales("v", wv_scales)
+        load_words(w_k, wk_words)
+        load_scales("k", wk_scales)
+        nc.sync.dma_start(
+            out=embt[:].rearrange("p r w j -> p r (w j)"),
+            in_=emb[0, 0].rearrange("(p r) c -> p r c", p=P),
+        )
+        load_x(0, 8, 16)
+        load_x(1, 0, 8)
+        load_x(1, 8, 16)
+
+        xw, xT, xs, xq, kvp, kvb, kvq, krp, kt, vt, outp = {}, {}, {}, {}, {}, {}, {}, {}, {}, {}, {}
+
+        def where(n):
+            return n // (R // PAIR), PAIR * (n % (R // PAIR))
+
+        def copy_out(which, out, in_):
+            if which in VECTOR_COPIES:
+                nc.vector.tensor_copy(out=out, in_=in_)
+            else:
+                nc.scalar.copy(out=out, in_=in_)
+
+        def widen(n):
+            b, r = where(n)
+            xw[n] = work.tile([P, PAIR, HID], BF16, name="xw", bufs=5)
+            src = xb[b][:, r : r + PAIR, :].bitcast(FP8)
+            if n in SCALAR_WIDENS:
+                nc.scalar.copy(out=xw[n][:], in_=src)
+            else:
+                nc.vector.tensor_copy(out=xw[n][:], in_=src)
+
+        def transposes(n):
+            xT[n] = psum.tile([P, 2, PAIR, P], F32, name="xT", bufs=2)
+            for l in range(PAIR):
+                words = xw[n][:, l, :].bitcast(F32)
+                for u in range(2):
+                    nc.tensor.transpose(xT[n][:, u, l, :], words[:, u : 256 : 2], ident[:])
+
+        def xscale(n):
+            xs[n] = work.tile([P, PAIR * P, 2, 2], BF16, name="xs", bufs=2, align_bytes=64)
+            nc.vector.tensor_tensor(
+                out=xs[n][:],
+                in0=xT[n][:].bitcast(BF16).rearrange("p u l (n e) -> p (l n) u e", e=2),
+                in1=xsc[:].rearrange("p (u e) -> p u e", u=2).unsqueeze(1).broadcast_to([P, PAIR * P, 2, 2]),
+                op=MULT,
+            )
+
+        def quantx(n):
+            codes = work.tile([P, PAIR * P], U32, name="xcodes", bufs=5, align_bytes=64)
+            scales = work.tile([P, PAIR * P], U8, name="xscales", bufs=5, align_bytes=64)
+            xq[n] = (codes, scales)
+            nc.vector.quantize_mx(
+                out=codes[:].bitcast(FP8X4), scales=scales[:],
+                in_=xs[n][:].rearrange("p n u e -> p (n u e)"),
+            )
+
+        def kv_matmuls(n):
+            codes, scales = xq[n]
+            kvp[n] = []
+            for l in range(PAIR):
+                cols = slice(l * P, (l + 1) * P)
+                bank = psum.tile([P, 4, P], F32, name="kvp", bufs=2)
+                kvp[n].append(bank)
+                for t in range(4):
+                    nc.tensor.matmul_mx(
+                        bank[:, t, :],
+                        lhsT=w_kv[:, 256 * t : 256 * (t + 1)].bitcast(FP4X4),
+                        lhsT_scale=s_kv[:, P * t : P * (t + 1)],
+                        rhs=codes[:, cols].bitcast(FP8X4),
+                        rhs_scale=scales[:, cols],
+                        start=True, stop=True,
+                    )
+
+        def kv_copies(n):
+            kvb[n] = work.tile([P, PAIR * P, 4], BF16, name="kvb", bufs=2, align_bytes=64)
+            for l in range(PAIR):
+                copy_out(
+                    ("kc", n, l),
+                    kvb[n][:, l * P : (l + 1) * P, :],
+                    kvp[n][l][:].rearrange("p t n -> p n t"),
+                )
+
+        def quantkv(n):
+            codes = work.tile([P, PAIR * P], U32, name="kcodes", bufs=2, align_bytes=64)
+            scales = work.tile([P, PAIR * P], U8, name="kscales", bufs=2, align_bytes=64)
+            kvq[n] = (codes, scales)
+            nc.vector.quantize_mx(
+                out=codes[:].bitcast(FP8X4), scales=scales[:],
+                in_=kvb[n][:].rearrange("p n t -> p (n t)"),
+            )
+
+        def token_matmul(out, q, l, words, which):
+            codes, scales = q
+            cols = slice(l * P, (l + 1) * P)
+            lo, hi = PL[which]
+            nc.tensor.matmul_mx(
+                out,
+                lhsT=codes[:, cols].bitcast(FP8X4), lhsT_scale=scales[:, cols],
+                rhs=words[:].bitcast(FP4X4), rhs_scale=planes[:, lo:hi],
+                start=True, stop=True,
+            )
+
+        def kr_matmuls(n):
+            krp[n] = psum.tile([P, PAIR, 2 * H, HALF], F32, name="krp", bufs=1)
+            for l in range(PAIR):
+                token_matmul(krp[n][:, l].rearrange("p g j -> p (g j)"), xq[n], l, w_r, "r")
+
+        def rope(n):
+            b, r = where(n)
+            kt[n] = work.tile([P, PAIR, H, HD], F32, name="kt", bufs=4)
+            m = work.tile([P, PAIR, 2 * H, 2, HALF], F32, name="m", bufs=2)
+            shape = [P, PAIR, 2 * H, 2, HALF]
+            nc.vector.tensor_tensor(
+                out=m[:],
+                in0=krp[n][:].unsqueeze(3).broadcast_to(shape),
+                in1=embt[:, r : r + PAIR].unsqueeze(2).broadcast_to(shape),
+                op=MULT,
+            )
+            mv = m[:].rearrange("p l (h a) w j -> p (l h) a w j", a=2)
+            ko = kt[n][:].rearrange("p l h d -> p (l h) d")
+            nc.gpsimd.tensor_tensor(
+                out=ko[:, :, ROT : ROT + HALF], in0=mv[:, :, 0, 1, :], in1=mv[:, :, 1, 0, :], op=SUB)
+            nc.gpsimd.tensor_tensor(
+                out=ko[:, :, ROT + HALF :], in0=mv[:, :, 1, 1, :], in1=mv[:, :, 0, 0, :], op=ADD)
+
+        def out_matmuls(n):
+            vt[n] = work.tile([P, PAIR, H * HD], F32, name="vt", bufs=4)
+            outp[n] = []
+            for l in range(PAIR):
+                bank = psum.tile([P, 512], F32, name="vp", bufs=2)
+                outp[n].append(bank)
+                token_matmul(bank[:], kvq[n], l, w_v, "v")
+            bank = psum.tile([P, PAIR, H, ROT], F32, name="kcp", bufs=1)
+            outp[n].append(bank)
+            for l in range(PAIR):
+                token_matmul(bank[:, l].rearrange("p h d -> p (h d)"), kvq[n], l, w_k, "k")
+
+        def out_copies(n):
+            for l in range(PAIR):
+                copy_out(("v", n, l), vt[n][:, l, :], outp[n][l][:])
+            copy_out(
+                ("k", n, 0),
+                kt[n][:].rearrange("p l h d -> p (l h) d")[:, :, 0:ROT],
+                outp[n][2][:].rearrange("p l h d -> p (l h) d"),
+            )
+
+        def store(n):
+            b, r = where(n)
+            nc.sync.dma_start(
+                out=v_out[b].rearrange("(p r) h d -> p r (h d)", p=P)[:, r : r + PAIR, :], in_=vt[n][:])
+            nc.sync.dma_start(
+                out=k_out[b].rearrange("(p r) h d -> p r (h d)", p=P)[:, r : r + PAIR, :],
+                in_=kt[n][:].rearrange("p l h d -> p l (h d)"))
+
+        def have(n):
+            return 0 <= n < NP
+
+        for i in range(-4, NP + 1):
+            if i == -3:
+                nc.vector.tensor_copy(
+                    out=w_kv[:].rearrange("p (t m c) -> p t m c", t=4, c=2),
+                    in_=w_kv_raw[:].rearrange("p (m t c) -> p t m c", t=4, c=2))
+                nc.vector.tensor_copy(
+                    out=s_kv[:].rearrange("p (t m) -> p t m", t=4),
+                    in_=planes[:, 0:512].rearrange("p (m t) -> p t m", t=4))
+            if have(i):
+                kv_matmuls(i)
+                kv_copies(i)
+            if have(i - 1):
+                rope(i - 1)
+            if have(i + 2):
+                xscale(i + 2)
+            if have(i - 1):
+                out_matmuls(i - 1)
+                out_copies(i - 1)
+            if have(i):
+                quantkv(i)
+            if have(i + 2):
+                quantx(i + 2)
+            if have(i):
+                kr_matmuls(i)
+            if have(i + 4):
+                widen(i + 4)
+            if have(i + 3):
+                transposes(i + 3)
+            if have(i - 1):
+                store(i - 1)

@@ -23,8 +23,8 @@ FLOPS = 2 * B * S * HID * (LAT + H * ROT + H * HD + H * ROT)
 
 PAIR = 2
 NP = B * R // PAIR
-SCALAR_WIDENS = (1, 2, 3, 5, 7, 9, 11, 13)
-VECTOR_COPIES = {("kc", 15, 0), ("v", 14, 0), ("v", 15, 0), ("k", 15, 0)}
+SCALAR_WIDENS = (1, 2, 4, 5, 6, 10, 12, 14)
+VECTOR_COPIES = {("kc", 15, 0), ("v", 13, 1), ("v", 15, 1)}
 
 
 def tile_llamaattention_pb_t_w4_kernel(
@@ -53,8 +53,13 @@ def tile_llamaattention_pb_t_w4_kernel(
         s_kv = keep.tile([P, 512], U8, align_bytes=64)
         w_v = keep.tile([P, 1024], U8, align_bytes=64)
         w_k = keep.tile([P, 512], U8, align_bytes=64)
+        w_r_raw = keep.tile([P, 512], U8, align_bytes=64)
         w_r = keep.tile([P, 512], U8, align_bytes=64)
+        s_r = keep.tile([P, 256], U8, align_bytes=64)
         embt = keep.tile([P, R, 2, HALF], BF16)
+        tab = keep.tile([P, R, 3, HALF], F32)
+        ones = keep.tile([P, 1], F32)
+        nc.vector.memset(ones[:], 1.0)
 
         def load_x(b, r0, r1):
             nc.sync.dma_start(out=xb[b][:, r0:r1, :], in_=x_view[b][:, r0:r1, :])
@@ -75,19 +80,23 @@ def tile_llamaattention_pb_t_w4_kernel(
         nc.sync.dma_start(out=xsc[:], in_=x_scale.rearrange("a b (p t) -> p (a b t)", t=4))
         load_words(w_kv_raw, wkv_words)
         load_scales("kv", wkv_scales)
-        load_words(w_r, wr_words)
-        load_scales("r", wr_scales)
-        load_words(w_v, wv_words)
-        load_scales("v", wv_scales)
-        load_words(w_k, wk_words)
-        load_scales("k", wk_scales)
         nc.sync.dma_start(
             out=embt[:].rearrange("p r w j -> p r (w j)"),
             in_=emb[0, 0].rearrange("(p r) c -> p r c", p=P),
         )
         load_x(0, 8, 16)
+        load_words(w_r_raw, wr_words)
+        load_scales("r", wr_scales)
+        load_words(w_v, wv_words)
+        load_scales("v", wv_scales)
+        load_words(w_k, wk_words)
+        load_scales("k", wk_scales)
         load_x(1, 0, 8)
         load_x(1, 8, 16)
+
+        sin, cos = embt[:, :, 0, :], embt[:, :, 1, :]
+        nc.gpsimd.tensor_tensor(out=tab[:, :, 1, :], in0=sin, in1=cos, op=SUB)
+        nc.gpsimd.tensor_tensor(out=tab[:, :, 2, :], in0=sin, in1=cos, op=ADD)
 
         xw, xT, xs, xq, kvp, kvb, kvq, krp, kt, vt, outp = {}, {}, {}, {}, {}, {}, {}, {}, {}, {}, {}
 
@@ -102,19 +111,29 @@ def tile_llamaattention_pb_t_w4_kernel(
 
         def widen(n):
             b, r = where(n)
-            xw[n] = work.tile([P, PAIR, HID], BF16, name="xw", bufs=5)
-            src = xb[b][:, r : r + PAIR, :].bitcast(FP8)
+            xw[n] = work.tile([P, PAIR * HID], BF16, name="xw", bufs=5)
+            src = xb[b][:, r : r + PAIR, :].bitcast(FP8).rearrange("p l k -> p (l k)")
             if n in SCALAR_WIDENS:
                 nc.scalar.copy(out=xw[n][:], in_=src)
             else:
-                nc.vector.tensor_copy(out=xw[n][:], in_=src)
+                nc.vector.tensor_scalar(
+                    out=xw[n][:].rearrange("p (u w e) -> p w u e", u=2, e=2),
+                    in0=src.rearrange("p (w u e) -> p w u e", u=2, e=2),
+                    scalar1=ones[:], scalar2=None, op0=MULT)
 
         def transposes(n):
-            xT[n] = psum.tile([P, 2, PAIR, P], F32, name="xT", bufs=2)
+            if n in (1, 2):
+                xT[n] = psum.tile([P, 2, PAIR, P], F32, name="xTv", tag="vp", bufs=2)
+            else:
+                xT[n] = psum.tile([P, 2, PAIR, P], F32, name="xT", tag="xT", bufs=1)
+            words = xw[n][:].bitcast(F32)
             for l in range(PAIR):
-                words = xw[n][:, l, :].bitcast(F32)
                 for u in range(2):
-                    nc.tensor.transpose(xT[n][:, u, l, :], words[:, u : 256 : 2], ident[:])
+                    if n in SCALAR_WIDENS:
+                        cols = words[:, 256 * l + u : 256 * (l + 1) : 2]
+                    else:
+                        cols = words[:, 256 * u + P * l : 256 * u + P * (l + 1)]
+                    nc.tensor.transpose(xT[n][:, u, l, :], cols, ident[:])
 
         def xscale(n):
             xs[n] = work.tile([P, PAIR * P, 2, 2], BF16, name="xs", bufs=2, align_bytes=64)
@@ -151,14 +170,16 @@ def tile_llamaattention_pb_t_w4_kernel(
                         start=True, stop=True,
                     )
 
-        def kv_copies(n):
-            kvb[n] = work.tile([P, PAIR * P, 4], BF16, name="kvb", bufs=2, align_bytes=64)
+        def kv_copies(n, engine):
+            if n not in kvb:
+                kvb[n] = work.tile([P, PAIR * P, 4], BF16, name="kvb", bufs=2, align_bytes=64)
             for l in range(PAIR):
-                copy_out(
-                    ("kc", n, l),
-                    kvb[n][:, l * P : (l + 1) * P, :],
-                    kvp[n][l][:].rearrange("p t n -> p n t"),
-                )
+                if (engine is nc.vector) == (("kc", n, l) in VECTOR_COPIES):
+                    copy_out(
+                        ("kc", n, l),
+                        kvb[n][:, l * P : (l + 1) * P, :],
+                        kvp[n][l][:].rearrange("p t n -> p n t"),
+                    )
 
         def quantkv(n):
             codes = work.tile([P, PAIR * P], U32, name="kcodes", bufs=2, align_bytes=64)
@@ -181,33 +202,46 @@ def tile_llamaattention_pb_t_w4_kernel(
             )
 
         def kr_matmuls(n):
-            krp[n] = psum.tile([P, PAIR, 2 * H, HALF], F32, name="krp", bufs=1)
+            krp[n] = []
+            codes, scales = xq[n]
             for l in range(PAIR):
-                token_matmul(krp[n][:, l].rearrange("p g j -> p (g j)"), xq[n], l, w_r, "r")
+                bank = psum.tile([P, 3, H, HALF], F32, name="krp", bufs=2)
+                krp[n].append(bank)
+                cols = slice(l * P, (l + 1) * P)
+                for out, lo, hi, start, stop in (
+                    (bank[:, 1:3].rearrange("p c h j -> p (c h j)"), 0, 256, True, True),
+                    (bank[:, 0].rearrange("p h j -> p (h j)"), 0, 128, True, False),
+                    (bank[:, 0].rearrange("p h j -> p (h j)"), 128, 256, False, True),
+                ):
+                    nc.tensor.matmul_mx(
+                        out,
+                        lhsT=codes[:, cols].bitcast(FP8X4), lhsT_scale=scales[:, cols],
+                        rhs=w_r[:, 2 * lo : 2 * hi].bitcast(FP4X4), rhs_scale=s_r[:, lo:hi],
+                        start=start, stop=stop,
+                    )
 
         def rope(n):
             b, r = where(n)
             kt[n] = work.tile([P, PAIR, H, HD], F32, name="kt", bufs=4)
-            m = work.tile([P, PAIR, 2 * H, 2, HALF], F32, name="m", bufs=2)
-            shape = [P, PAIR, 2 * H, 2, HALF]
-            nc.vector.tensor_tensor(
-                out=m[:],
-                in0=krp[n][:].unsqueeze(3).broadcast_to(shape),
-                in1=embt[:, r : r + PAIR].unsqueeze(2).broadcast_to(shape),
-                op=MULT,
-            )
-            mv = m[:].rearrange("p l (h a) w j -> p (l h) a w j", a=2)
-            ko = kt[n][:].rearrange("p l h d -> p (l h) d")
+            m = work.tile([P, PAIR, 3, H, HALF], F32, name="m", bufs=2)
+            shape = [P, 3, H, HALF]
+            for l in range(PAIR):
+                nc.vector.tensor_tensor(
+                    out=m[:, l], in0=krp[n][l][:],
+                    in1=tab[:, r + l].unsqueeze(2).broadcast_to(shape),
+                    op=MULT,
+                )
+            ko = kt[n][:]
             nc.gpsimd.tensor_tensor(
-                out=ko[:, :, ROT : ROT + HALF], in0=mv[:, :, 0, 1, :], in1=mv[:, :, 1, 0, :], op=SUB)
+                out=ko[:, :, :, ROT : ROT + HALF], in0=m[:, :, 0], in1=m[:, :, 2], op=SUB)
             nc.gpsimd.tensor_tensor(
-                out=ko[:, :, ROT + HALF :], in0=mv[:, :, 1, 1, :], in1=mv[:, :, 0, 0, :], op=ADD)
+                out=ko[:, :, :, ROT + HALF :], in0=m[:, :, 0], in1=m[:, :, 1], op=ADD)
 
         def out_matmuls(n):
             vt[n] = work.tile([P, PAIR, H * HD], F32, name="vt", bufs=4)
             outp[n] = []
             for l in range(PAIR):
-                bank = psum.tile([P, 512], F32, name="vp", bufs=2)
+                bank = psum.tile([P, 512], F32, name="vp", tag="vp", bufs=2)
                 outp[n].append(bank)
                 token_matmul(bank[:], kvq[n], l, w_v, "v")
             bank = psum.tile([P, PAIR, H, ROT], F32, name="kcp", bufs=1)
@@ -226,11 +260,14 @@ def tile_llamaattention_pb_t_w4_kernel(
 
         def store(n):
             b, r = where(n)
-            nc.sync.dma_start(
-                out=v_out[b].rearrange("(p r) h d -> p r (h d)", p=P)[:, r : r + PAIR, :], in_=vt[n][:])
-            nc.sync.dma_start(
-                out=k_out[b].rearrange("(p r) h d -> p r (h d)", p=P)[:, r : r + PAIR, :],
-                in_=kt[n][:].rearrange("p l h d -> p l (h d)"))
+            vo = v_out[b].rearrange("(p r) h d -> p r (h d)", p=P)
+            ko = k_out[b].rearrange("(p r) h d -> p r (h d)", p=P)
+            for l0, l1 in ((0, 1), (1, 2)) if n == NP - 1 else ((0, PAIR),):
+                nc.sync.dma_start(out=vo[:, r + l0 : r + l1, :], in_=vt[n][:, l0:l1])
+            for l0, l1 in ((0, 1), (1, 2)) if n == NP - 1 else ((0, PAIR),):
+                nc.sync.dma_start(
+                    out=ko[:, r + l0 : r + l1, :],
+                    in_=kt[n][:, l0:l1].rearrange("p l h d -> p l (h d)"))
 
         def have(n):
             return 0 <= n < NP
@@ -243,25 +280,38 @@ def tile_llamaattention_pb_t_w4_kernel(
                 nc.vector.tensor_copy(
                     out=s_kv[:].rearrange("p (t m) -> p t m", t=4),
                     in_=planes[:, 0:512].rearrange("p (m t) -> p t m", t=4))
-            if have(i):
-                kv_matmuls(i)
-                kv_copies(i)
             if have(i - 1):
                 rope(i - 1)
-            if have(i + 2):
-                xscale(i + 2)
             if have(i - 1):
                 out_matmuls(i - 1)
+            if have(i + 2):
+                xscale(i + 2)
+            if have(i):
+                kv_copies(i, nc.vector)
+            if have(i + 4):
+                widen(i + 4)
+            if have(i):
+                kv_copies(i, nc.scalar)
+            if i == -1:
+                nc.scalar.copy(out=tab[:, :, 0, :], in_=cos)
+            if have(i - 1):
                 out_copies(i - 1)
             if have(i):
                 quantkv(i)
-            if have(i + 2):
-                quantx(i + 2)
+            if i == 0:
+                nc.vector.tensor_copy(
+                    out=w_r[:].bitcast(I32).rearrange("p (a h c) -> p a h c", a=2, h=H),
+                    in_=w_r_raw[:].bitcast(I32).rearrange("p (h a c) -> p a h c", a=2, h=H))
+                nc.vector.tensor_copy(
+                    out=s_r[:].bitcast(I32).rearrange("p (a h c) -> p a h c", a=2, h=H),
+                    in_=planes[:, 1280:1536].bitcast(I32).rearrange("p (h a c) -> p a h c", a=2, h=H))
             if have(i):
                 kr_matmuls(i)
-            if have(i + 4):
-                widen(i + 4)
+            if have(i + 1):
+                kv_matmuls(i + 1)
             if have(i + 3):
                 transposes(i + 3)
+            if have(i + 2):
+                quantx(i + 2)
             if have(i - 1):
                 store(i - 1)

@@ -23,8 +23,8 @@ FLOPS = 2 * B * S * HID * (LAT + H * ROT + H * HD + H * ROT)
 
 PAIR = 2
 NP = B * R // PAIR
-SCALAR_WIDENS = (1, 2, 4, 5, 6, 10, 12, 14)
-VECTOR_COPIES = {("kc", 15, 0), ("v", 13, 1), ("v", 15, 1)}
+SCALAR_WIDENS = (1, 2, 3, 4, 5, 7, 10)
+VECTOR_COPIES = {("kc", 14, 1), ("v", 13, 1), ("v", 14, 1), ("v", 15, 0), ("k", 15, 0)}
 
 
 def tile_llamaattention_pb_t_w4_kernel(
@@ -38,8 +38,6 @@ def tile_llamaattention_pb_t_w4_kernel(
         psum = ctx.enter_context(tc.psum_pool(name="psum", bufs=1))
         ctx.enter_context(tc.manual_schedule())
 
-        ident = keep.tile([P, P], F32)
-        make_identity(nc, ident[:])
 
         planes = keep.tile([P, 1536], U8, align_bytes=64)
         nc.vector.memset(planes[:].bitcast(I32), 0)
@@ -58,8 +56,14 @@ def tile_llamaattention_pb_t_w4_kernel(
         s_r = keep.tile([P, 256], U8, align_bytes=64)
         embt = keep.tile([P, R, 2, HALF], BF16)
         tab = keep.tile([P, R, 3, HALF], F32)
-        ones = keep.tile([P, 1], F32)
-        nc.vector.memset(ones[:], 1.0)
+
+        nc.gpsimd.dma_start(out=xsc[:], in_=x_scale.rearrange("a b (p t) -> p (a b t)", t=4))
+        ident = keep.tile([P, P], F32)
+        make_identity(nc, ident[:])
+        nc.gpsimd.dma_start(
+            out=embt[:].rearrange("p r w j -> p r (w j)"),
+            in_=emb[0, 0].rearrange("(p r) c -> p r c", p=P),
+        )
 
         def load_x(b, r0, r1):
             nc.sync.dma_start(out=xb[b][:, r0:r1, :], in_=x_view[b][:, r0:r1, :])
@@ -76,19 +80,15 @@ def tile_llamaattention_pb_t_w4_kernel(
                 )
 
         load_x(0, 0, 2)
-        load_x(0, 2, 8)
-        nc.sync.dma_start(out=xsc[:], in_=x_scale.rearrange("a b (p t) -> p (a b t)", t=4))
         load_words(w_kv_raw, wkv_words)
         load_scales("kv", wkv_scales)
-        nc.sync.dma_start(
-            out=embt[:].rearrange("p r w j -> p r (w j)"),
-            in_=emb[0, 0].rearrange("(p r) c -> p r c", p=P),
-        )
-        load_x(0, 8, 16)
-        load_words(w_r_raw, wr_words)
-        load_scales("r", wr_scales)
+        load_x(0, 2, 4)
+        load_x(0, 4, 8)
         load_words(w_v, wv_words)
         load_scales("v", wv_scales)
+        load_words(w_r_raw, wr_words)
+        load_x(0, 8, 16)
+        load_scales("r", wr_scales)
         load_words(w_k, wk_words)
         load_scales("k", wk_scales)
         load_x(1, 0, 8)
@@ -98,7 +98,7 @@ def tile_llamaattention_pb_t_w4_kernel(
         nc.gpsimd.tensor_tensor(out=tab[:, :, 1, :], in0=sin, in1=cos, op=SUB)
         nc.gpsimd.tensor_tensor(out=tab[:, :, 2, :], in0=sin, in1=cos, op=ADD)
 
-        xw, xT, xs, xq, kvp, kvb, kvq, krp, kt, vt, outp = {}, {}, {}, {}, {}, {}, {}, {}, {}, {}, {}
+        xw, xT, xs, xq, kvp, kvb, kvq, krp, kt, vt, outp, m = {}, {}, {}, {}, {}, {}, {}, {}, {}, {}, {}, {}
 
         def where(n):
             return n // (R // PAIR), PAIR * (n % (R // PAIR))
@@ -116,10 +116,7 @@ def tile_llamaattention_pb_t_w4_kernel(
             if n in SCALAR_WIDENS:
                 nc.scalar.copy(out=xw[n][:], in_=src)
             else:
-                nc.vector.tensor_scalar(
-                    out=xw[n][:].rearrange("p (u w e) -> p w u e", u=2, e=2),
-                    in0=src.rearrange("p (w u e) -> p w u e", u=2, e=2),
-                    scalar1=ones[:], scalar2=None, op0=MULT)
+                nc.vector.tensor_copy(out=xw[n][:], in_=src)
 
         def transposes(n):
             if n in (1, 2):
@@ -129,10 +126,7 @@ def tile_llamaattention_pb_t_w4_kernel(
             words = xw[n][:].bitcast(F32)
             for l in range(PAIR):
                 for u in range(2):
-                    if n in SCALAR_WIDENS:
-                        cols = words[:, 256 * l + u : 256 * (l + 1) : 2]
-                    else:
-                        cols = words[:, 256 * u + P * l : 256 * u + P * (l + 1)]
+                    cols = words[:, 256 * l + u : 256 * (l + 1) : 2]
                     nc.tensor.transpose(xT[n][:, u, l, :], cols, ident[:])
 
         def xscale(n):
@@ -170,16 +164,14 @@ def tile_llamaattention_pb_t_w4_kernel(
                         start=True, stop=True,
                     )
 
-        def kv_copies(n, engine):
-            if n not in kvb:
+        def kv_copy(n, l):
+            if l == 0:
                 kvb[n] = work.tile([P, PAIR * P, 4], BF16, name="kvb", bufs=2, align_bytes=64)
-            for l in range(PAIR):
-                if (engine is nc.vector) == (("kc", n, l) in VECTOR_COPIES):
-                    copy_out(
-                        ("kc", n, l),
-                        kvb[n][:, l * P : (l + 1) * P, :],
-                        kvp[n][l][:].rearrange("p t n -> p n t"),
-                    )
+            copy_out(
+                ("kc", n, l),
+                kvb[n][:, l * P : (l + 1) * P, :],
+                kvp[n][l][:].rearrange("p t n -> p n t"),
+            )
 
         def quantkv(n):
             codes = work.tile([P, PAIR * P], U32, name="kcodes", bufs=2, align_bytes=64)
@@ -220,22 +212,23 @@ def tile_llamaattention_pb_t_w4_kernel(
                         start=start, stop=stop,
                     )
 
-        def rope(n):
+        def rope_product(n, l):
             b, r = where(n)
+            if l == 0:
+                m[n] = work.tile([P, PAIR, 3, H, HALF], F32, name="m", bufs=3)
+            nc.vector.tensor_tensor(
+                out=m[n][:, l], in0=krp[n][l][:],
+                in1=tab[:, r + l].unsqueeze(2).broadcast_to([P, 3, H, HALF]),
+                op=MULT,
+            )
+
+        def rope_sums(n):
             kt[n] = work.tile([P, PAIR, H, HD], F32, name="kt", bufs=4)
-            m = work.tile([P, PAIR, 3, H, HALF], F32, name="m", bufs=2)
-            shape = [P, 3, H, HALF]
-            for l in range(PAIR):
-                nc.vector.tensor_tensor(
-                    out=m[:, l], in0=krp[n][l][:],
-                    in1=tab[:, r + l].unsqueeze(2).broadcast_to(shape),
-                    op=MULT,
-                )
-            ko = kt[n][:]
+            ko, mv = kt[n][:], m[n][:]
             nc.gpsimd.tensor_tensor(
-                out=ko[:, :, :, ROT : ROT + HALF], in0=m[:, :, 0], in1=m[:, :, 2], op=SUB)
+                out=ko[:, :, :, ROT : ROT + HALF], in0=mv[:, :, 0], in1=mv[:, :, 2], op=SUB)
             nc.gpsimd.tensor_tensor(
-                out=ko[:, :, :, ROT + HALF :], in0=m[:, :, 0], in1=m[:, :, 1], op=ADD)
+                out=ko[:, :, :, ROT + HALF :], in0=mv[:, :, 0], in1=mv[:, :, 1], op=ADD)
 
         def out_matmuls(n):
             vt[n] = work.tile([P, PAIR, H * HD], F32, name="vt", bufs=4)
@@ -280,24 +273,33 @@ def tile_llamaattention_pb_t_w4_kernel(
                 nc.vector.tensor_copy(
                     out=s_kv[:].rearrange("p (t m) -> p t m", t=4),
                     in_=planes[:, 0:512].rearrange("p (m t) -> p t m", t=4))
-            if have(i - 1):
-                rope(i - 1)
-            if have(i - 1):
-                out_matmuls(i - 1)
+            if have(i):
+                kv_copy(i, 0)
             if have(i + 2):
                 xscale(i + 2)
             if have(i):
-                kv_copies(i, nc.vector)
+                kv_copy(i, 1)
+            if have(i - 1):
+                out_matmuls(i - 1)
+            if have(i - 1) and i < NP:
+                rope_product(i - 1, 0)
             if have(i + 4):
                 widen(i + 4)
-            if have(i):
-                kv_copies(i, nc.scalar)
             if i == -1:
                 nc.scalar.copy(out=tab[:, :, 0, :], in_=cos)
-            if have(i - 1):
-                out_copies(i - 1)
+            if have(i + 2):
+                quantx(i + 2)
+            if have(i + 3):
+                transposes(i + 3)
+            if have(i - 1) and i < NP:
+                rope_product(i - 1, 1)
+                rope_sums(i - 1)
             if have(i):
                 quantkv(i)
+            if have(i + 1):
+                kv_matmuls(i + 1)
+            if have(i - 1):
+                out_copies(i - 1)
             if i == 0:
                 nc.vector.tensor_copy(
                     out=w_r[:].bitcast(I32).rearrange("p (a h c) -> p a h c", a=2, h=H),
@@ -307,11 +309,9 @@ def tile_llamaattention_pb_t_w4_kernel(
                     in_=planes[:, 1280:1536].bitcast(I32).rearrange("p (h a c) -> p a h c", a=2, h=H))
             if have(i):
                 kr_matmuls(i)
-            if have(i + 1):
-                kv_matmuls(i + 1)
-            if have(i + 3):
-                transposes(i + 3)
-            if have(i + 2):
-                quantx(i + 2)
+            if i == NP - 1:
+                rope_product(i, 0)
+                rope_product(i, 1)
+                rope_sums(i)
             if have(i - 1):
                 store(i - 1)

from contextlib import ExitStack

import concourse.mybir as mybir
from concourse.masks import make_identity

F32 = mybir.dt.float32
BF16 = mybir.dt.bfloat16
I32 = mybir.dt.int32
U32 = mybir.dt.uint32
U8 = mybir.dt.uint8
FP8 = mybir.dt.float8_e4m3fn
FP8X4 = mybir.dt.float8_e4m3fn_x4
FP4X4 = mybir.dt.float4_e2m1fn_x4
ADD = mybir.AluOpType.add
SUB = mybir.AluOpType.subtract
MULT = mybir.AluOpType.mult

B, S, H, HD, HID, LAT = 2, 2048, 4, 128, 512, 512
ROT, HALF = 64, 32
P = 128
R = S // P
FLOPS = 2 * B * S * HID * (LAT + H * ROT + H * HD + H * ROT)

PAIR = 2
NP = B * R // PAIR
SCALAR_WIDENS = (1, 2, 3, 4, 5, 7, 10)
VECTOR_COPIES = {("kc", 14, 1), ("v", 13, 1), ("v", 14, 1), ("v", 15, 0), ("k", 15, 0)}


def tile_llamaattention_pb_t_w4_kernel(
    tc, x_bytes, x_scale, emb, wkv_words, wkv_scales, wk_words, wk_scales,
    wv_words, wv_scales, wr_words, wr_scales, k_out, v_out,
):
    nc = tc.nc
    with ExitStack() as ctx:
        keep = ctx.enter_context(tc.tile_pool(name="keep", bufs=1))
        work = ctx.enter_context(tc.tile_pool(name="work", bufs=3))
        psum = ctx.enter_context(tc.psum_pool(name="psum", bufs=1))
        ctx.enter_context(tc.manual_schedule())


        planes = keep.tile([P, 1536], U8, align_bytes=64)
        nc.vector.memset(planes[:].bitcast(I32), 0)
        PL = {"kv": (0, 512), "v": (512, 1024), "k": (1024, 1280), "r": (1280, 1536)}

        xb = [keep.tile([P, R, HID], U8, name="xb%d" % b) for b in range(B)]
        x_view = [x_bytes[b].rearrange("(p r) k -> p r k", p=P) for b in range(B)]
        xsc = keep.tile([P, 4], F32)
        w_kv_raw = keep.tile([P, 1024], U8, align_bytes=64)
        w_kv = keep.tile([P, 1024], U8, align_bytes=64)
        s_kv = keep.tile([P, 512], U8, align_bytes=64)
        w_v = keep.tile([P, 1024], U8, align_bytes=64)
        w_k = keep.tile([P, 512], U8, align_bytes=64)
        w_r_raw = keep.tile([P, 512], U8, align_bytes=64)
        w_r = keep.tile([P, 512], U8, align_bytes=64)
        s_r = keep.tile([P, 256], U8, align_bytes=64)
        embt = keep.tile([P, R, 2, HALF], BF16)
        tab = keep.tile([P, R, 3, HALF], F32)

        nc.gpsimd.dma_start(out=xsc[:], in_=x_scale.rearrange("a b (p t) -> p (a b t)", t=4))
        ident = keep.tile([P, P], F32)
        make_identity(nc, ident[:])
        nc.gpsimd.dma_start(
            out=embt[:].rearrange("p r w j -> p r (w j)"),
            in_=emb[0, 0].rearrange("(p r) c -> p r c", p=P),
        )

        def load_x(b, r0, r1):
            nc.sync.dma_start(out=xb[b][:, r0:r1, :], in_=x_view[b][:, r0:r1, :])

        def load_words(tile, src):
            nc.sync.dma_start(out=tile[:].bitcast(I32), in_=src[0].bitcast(I32))

        def load_scales(which, src):
            lo, hi = PL[which]
            for q in range(4):
                nc.sync.dma_start(
                    out=planes[32 * q : 32 * q + 4, lo:hi].bitcast(I32),
                    in_=src[0, 4 * q : 4 * q + 4, :].bitcast(I32),
                )

        load_x(0, 0, 2)
        load_words(w_kv_raw, wkv_words)
        load_scales("kv", wkv_scales)
        load_x(0, 2, 4)
        load_x(0, 4, 8)
        load_words(w_v, wv_words)
        load_scales("v", wv_scales)
        load_words(w_r_raw, wr_words)
        load_x(0, 8, 16)
        load_scales("r", wr_scales)
        load_words(w_k, wk_words)
        load_scales("k", wk_scales)
        load_x(1, 0, 8)
        load_x(1, 8, 16)

        sin, cos = embt[:, :, 0, :], embt[:, :, 1, :]
        nc.gpsimd.tensor_tensor(out=tab[:, :, 1, :], in0=sin, in1=cos, op=SUB)
        nc.gpsimd.tensor_tensor(out=tab[:, :, 2, :], in0=sin, in1=cos, op=ADD)

        xw, xT, xs, xq, kvp, kvb, kvq, krp, kt, vt, outp, m = {}, {}, {}, {}, {}, {}, {}, {}, {}, {}, {}, {}

        def where(n):
            return n // (R // PAIR), PAIR * (n % (R // PAIR))

        def copy_out(which, out, in_):
            if which in VECTOR_COPIES:
                nc.vector.tensor_copy(out=out, in_=in_)
            else:
                nc.scalar.copy(out=out, in_=in_)

        def widen(n):
            b, r = where(n)
            xw[n] = work.tile([P, PAIR * HID], BF16, name="xw", bufs=5)
            src = xb[b][:, r : r + PAIR, :].bitcast(FP8).rearrange("p l k -> p (l k)")
            if n in SCALAR_WIDENS:
                nc.scalar.copy(out=xw[n][:], in_=src)
            else:
                nc.vector.tensor_copy(out=xw[n][:], in_=src)

        def transposes(n):
            if n in (1, 2):
                xT[n] = psum.tile([P, 2, PAIR, P], F32, name="xTv", tag="vp", bufs=2)
            else:
                xT[n] = psum.tile([P, 2, PAIR, P], F32, name="xT", tag="xT", bufs=1)
            words = xw[n][:].bitcast(F32)
            for l in range(PAIR):
                for u in range(2):
                    cols = words[:, 256 * l + u : 256 * (l + 1) : 2]
                    nc.tensor.transpose(xT[n][:, u, l, :], cols, ident[:])

        def xscale(n):
            xs[n] = work.tile([P, PAIR * P, 2, 2], BF16, name="xs", bufs=2, align_bytes=64)
            nc.vector.tensor_tensor(
                out=xs[n][:],
                in0=xT[n][:].bitcast(BF16).rearrange("p u l (n e) -> p (l n) u e", e=2),
                in1=xsc[:].rearrange("p (u e) -> p u e", u=2).unsqueeze(1).broadcast_to([P, PAIR * P, 2, 2]),
                op=MULT,
            )

        def quantx(n):
            codes = work.tile([P, PAIR * P], U32, name="xcodes", bufs=5, align_bytes=64)
            scales = work.tile([P, PAIR * P], U8, name="xscales", bufs=5, align_bytes=64)
            xq[n] = (codes, scales)
            nc.vector.quantize_mx(
                out=codes[:].bitcast(FP8X4), scales=scales[:],
                in_=xs[n][:].rearrange("p n u e -> p (n u e)"),
            )

        def kv_matmuls(n):
            codes, scales = xq[n]
            kvp[n] = []
            for l in range(PAIR):
                cols = slice(l * P, (l + 1) * P)
                bank = psum.tile([P, 4, P], F32, name="kvp", bufs=2)
                kvp[n].append(bank)
                for t in range(4):
                    nc.tensor.matmul_mx(
                        bank[:, t, :],
                        lhsT=w_kv[:, 256 * t : 256 * (t + 1)].bitcast(FP4X4),
                        lhsT_scale=s_kv[:, P * t : P * (t + 1)],
                        rhs=codes[:, cols].bitcast(FP8X4),
                        rhs_scale=scales[:, cols],
                        start=True, stop=True,
                    )

        def kv_copy(n, l):
            if l == 0:
                kvb[n] = work.tile([P, PAIR * P, 4], BF16, name="kvb", bufs=2, align_bytes=64)
            copy_out(
                ("kc", n, l),
                kvb[n][:, l * P : (l + 1) * P, :],
                kvp[n][l][:].rearrange("p t n -> p n t"),
            )

        def quantkv(n):
            codes = work.tile([P, PAIR * P], U32, name="kcodes", bufs=2, align_bytes=64)
            scales = work.tile([P, PAIR * P], U8, name="kscales", bufs=2, align_bytes=64)
            kvq[n] = (codes, scales)
            nc.vector.quantize_mx(
                out=codes[:].bitcast(FP8X4), scales=scales[:],
                in_=kvb[n][:].rearrange("p n t -> p (n t)"),
            )

        def token_matmul(out, q, l, words, which):
            codes, scales = q
            cols = slice(l * P, (l + 1) * P)
            lo, hi = PL[which]
            nc.tensor.matmul_mx(
                out,
                lhsT=codes[:, cols].bitcast(FP8X4), lhsT_scale=scales[:, cols],
                rhs=words[:].bitcast(FP4X4), rhs_scale=planes[:, lo:hi],
                start=True, stop=True,
            )

        def kr_matmuls(n):
            krp[n] = []
            codes, scales = xq[n]
            for l in range(PAIR):
                bank = psum.tile([P, 3, H, HALF], F32, name="krp", bufs=2)
                krp[n].append(bank)
                cols = slice(l * P, (l + 1) * P)
                for out, lo, hi, start, stop in (
                    (bank[:, 1:3].rearrange("p c h j -> p (c h j)"), 0, 256, True, True),
                    (bank[:, 0].rearrange("p h j -> p (h j)"), 0, 128, True, False),
                    (bank[:, 0].rearrange("p h j -> p (h j)"), 128, 256, False, True),
                ):
                    nc.tensor.matmul_mx(
                        out,
                        lhsT=codes[:, cols].bitcast(FP8X4), lhsT_scale=scales[:, cols],
                        rhs=w_r[:, 2 * lo : 2 * hi].bitcast(FP4X4), rhs_scale=s_r[:, lo:hi],
                        start=start, stop=stop,
                    )

        def rope_product(n, l):
            b, r = where(n)
            if l == 0:
                m[n] = work.tile([P, PAIR, 3, H, HALF], F32, name="m", bufs=3)
            nc.vector.tensor_tensor(
                out=m[n][:, l], in0=krp[n][l][:],
                in1=tab[:, r + l].unsqueeze(2).broadcast_to([P, 3, H, HALF]),
                op=MULT,
            )

        def rope_sums(n):
            kt[n] = work.tile([P, PAIR, H, HD], F32, name="kt", bufs=4)
            ko, mv = kt[n][:], m[n][:]
            nc.gpsimd.tensor_tensor(
                out=ko[:, :, :, ROT : ROT + HALF], in0=mv[:, :, 0], in1=mv[:, :, 2], op=SUB)
            nc.gpsimd.tensor_tensor(
                out=ko[:, :, :, ROT + HALF :], in0=mv[:, :, 0], in1=mv[:, :, 1], op=ADD)

        def out_matmuls(n):
            vt[n] = work.tile([P, PAIR, H * HD], F32, name="vt", bufs=4)
            outp[n] = []
            for l in range(PAIR):
                bank = psum.tile([P, 512], F32, name="vp", tag="vp", bufs=2)
                outp[n].append(bank)
                token_matmul(bank[:], kvq[n], l, w_v, "v")
            bank = psum.tile([P, PAIR, H, ROT], F32, name="kcp", bufs=1)
            outp[n].append(bank)
            for l in range(PAIR):
                token_matmul(bank[:, l].rearrange("p h d -> p (h d)"), kvq[n], l, w_k, "k")

        def out_copies(n):
            for l in range(PAIR):
                copy_out(("v", n, l), vt[n][:, l, :], outp[n][l][:])
            copy_out(
                ("k", n, 0),
                kt[n][:].rearrange("p l h d -> p (l h) d")[:, :, 0:ROT],
                outp[n][2][:].rearrange("p l h d -> p (l h) d"),
            )

        def store(n):
            b, r = where(n)
            vo = v_out[b].rearrange("(p r) h d -> p r (h d)", p=P)
            ko = k_out[b].rearrange("(p r) h d -> p r (h d)", p=P)
            for l0, l1 in ((0, 1), (1, 2)) if n == NP - 1 else ((0, PAIR),):
                nc.sync.dma_start(out=vo[:, r + l0 : r + l1, :], in_=vt[n][:, l0:l1])
            for l0, l1 in ((0, 1), (1, 2)) if n == NP - 1 else ((0, PAIR),):
                nc.sync.dma_start(
                    out=ko[:, r + l0 : r + l1, :],
                    in_=kt[n][:, l0:l1].rearrange("p l h d -> p l (h d)"))

        def have(n):
            return 0 <= n < NP

        for i in range(-4, NP + 1):
            if i == -3:
                nc.vector.tensor_copy(
                    out=w_kv[:].rearrange("p (t m c) -> p t m c", t=4, c=2),
                    in_=w_kv_raw[:].rearrange("p (m t c) -> p t m c", t=4, c=2))
                nc.vector.tensor_copy(
                    out=s_kv[:].rearrange("p (t m) -> p t m", t=4),
                    in_=planes[:, 0:512].rearrange("p (m t) -> p t m", t=4))
            if have(i):
                kv_copy(i, 0)
            if have(i + 2):
                xscale(i + 2)
            if have(i):
                kv_copy(i, 1)
            if have(i - 1):
                out_matmuls(i - 1)
            if have(i - 1) and i < NP:
                rope_product(i - 1, 0)
            if have(i + 4):
                widen(i + 4)
            if i == -1:
                nc.scalar.copy(out=tab[:, :, 0, :], in_=cos)
            if have(i + 2):
                quantx(i + 2)
            if have(i + 3):
                transposes(i + 3)
            if have(i - 1) and i < NP:
                rope_product(i - 1, 1)
                rope_sums(i - 1)
            if have(i):
                quantkv(i)
            if have(i + 1):
                kv_matmuls(i + 1)
            if have(i - 1):
                out_copies(i - 1)
            if i == 0:
                nc.vector.tensor_copy(
                    out=w_r[:].bitcast(I32).rearrange("p (a h c) -> p a h c", a=2, h=H),
                    in_=w_r_raw[:].bitcast(I32).rearrange("p (h a c) -> p a h c", a=2, h=H))
                nc.vector.tensor_copy(
                    out=s_r[:].bitcast(I32).rearrange("p (a h c) -> p a h c", a=2, h=H),
                    in_=planes[:, 1280:1536].bitcast(I32).rearrange("p (h a c) -> p a h c", a=2, h=H))
            if have(i):
                kr_matmuls(i)
            if i == NP - 1:
                rope_product(i, 0)
                rope_product(i, 1)
                rope_sums(i)
            if have(i - 1):
                store(i - 1)
